import numpy as np
import ml_dtypes


def mxq(x, axis, fmt="e4m3"):
    dtype, down = {"e4m3": (ml_dtypes.float8_e4m3fn, 7), "e5m2": (ml_dtypes.float8_e5m2, 14)}[fmt]
    v = np.moveaxis(np.asarray(x, np.float32).astype(ml_dtypes.bfloat16).astype(np.float64), axis, -1)
    blocks = v.reshape(v.shape[:-1] + (-1, 32))
    amax = np.abs(blocks).max(-1, keepdims=True)
    byte = np.maximum(np.where(amax > 0, np.frexp(amax)[1] - 1 + 127, 0) - down, 1)
    scale = np.exp2(byte - 127.0)
    codes = (blocks / scale).astype(np.float32).astype(dtype).astype(np.float64)
    return np.moveaxis((codes * scale).reshape(v.shape), -1, axis)


WIDE = False


def mx_kscale(k):
    if not WIDE:
        return np.ones(k)
    levels = np.array([10, -10, 5, -5, 0])
    a = np.random.permutation(np.resize(levels, k // 512 * 4)).reshape(k // 512, 4)
    idx = np.arange(k)
    return np.exp2(a[idx // 512, idx % 128 // 32])


BF16 = ml_dtypes.bfloat16


def bf(x):
    return np.asarray(x, np.float32).astype(BF16)


def f64(x):
    return np.asarray(x).astype(np.float64)


N, B, A, C, D, NR, XD = 4, 1024, 512, 64, 1024, 8, 3
GAMMA = 6.125


def setup_inputs():
    s = mx_kscale(A)
    t = mx_kscale(C * NR)[::NR]
    return {"input": bf(np.exp(np.random.standard_normal((N, C, A))) * 16.0 / A * s * t[:, None]),
            "difference_mat": bf(np.random.standard_normal((N, B, A, XD))),
            "relative_mask": bf(np.random.random((N, B, A)) / s),
            "W": bf(np.random.standard_normal((D, C, NR)) / np.sqrt(C * NR) / t[:, None]),
            "radii": bf(np.random.random(NR) * 2.0)}


def reference(input, difference_mat, relative_mask, W, radii):
    dm = f64(difference_mat)
    dist = np.sqrt(np.sum(dm * dm, axis=-1))
    R = np.exp(-GAMMA * (dist[..., None] - f64(radii)) ** 2)
    R = R * f64(relative_mask)[..., None]
    Rk = R.transpose(0, 2, 1, 3).reshape(N, A, B * NR)
    T = mxq(f64(input), 2, "e4m3") @ mxq(Rk, 1, "e4m3")
    Tk = T.reshape(N, C, B, NR).transpose(0, 1, 3, 2).reshape(N, C * NR, B)
    return mxq(f64(W).reshape(D, C * NR), 1, "e4m3") @ mxq(Tk, 1, "e4m3")

@@ -1,0 +1,322 @@
+from contextlib import ExitStack
+
+import concourse.bass as bass
+import concourse.mybir as mybir
+import concourse.tile as tile
+from concourse.masks import make_identity
+
+F32 = mybir.dt.float32
+BF16 = mybir.dt.bfloat16
+U32 = mybir.dt.uint32
+U8 = mybir.dt.uint8
+I32 = mybir.dt.int32
+FP8X4 = mybir.dt.float8_e4m3fn_x4
+ACT = mybir.ActivationFunctionType
+ALU = mybir.AluOpType
+
+NCLOUD, B, A, C, D, NR, XD = 4, 1024, 512, 64, 1024, 8, 3
+GAMMA = 6.125
+P = 128
+NT = A // P
+CH = 128
+CPN = B // CH
+NCH = NCLOUD * CPN
+COLS = CH * NT
+S_RADII = 5
+FLOPS = 2 * NCLOUD * C * A * B * NR + 2 * NCLOUD * D * C * NR * B
+
+
+def tile_se3pointconvolution_t_kernel(tc, feat, diff, mask, w, radii, out):
+    nc = tc.nc
+    with ExitStack() as ctx:
+        ctx.enter_context(tc.manual_schedule())
+        const = ctx.enter_context(tc.tile_pool(name="const", bufs=1))
+        dpool = ctx.enter_context(tc.tile_pool(name="dist", bufs=1))
+        keep = ctx.enter_context(tc.tile_pool(name="keep", bufs=1))
+        stage = ctx.enter_context(tc.tile_pool(name="stage", bufs=2))
+        mraw_pool = ctx.enter_context(tc.tile_pool(name="mraw", bufs=3))
+
+        one = const.tile([P, 1], F32, name="one")
+        junk = const.tile([P, 1], F32, name="junk")
+        rad_b = const.tile([P, NR], BF16, name="rad_b")
+        negr = const.tile([P, NR], F32, name="negr")
+        ident_f = const.tile([P, P], F32, name="ident_f")
+        ident_b = const.tile([P, P], BF16, name="ident_b")
+        nc.scalar.dma_start(out=rad_b[:], in_=radii.partition_broadcast(P))
+        nc.vector.memset(one[:], 1.0)
+        nc.scalar.activation(out=junk[:], in_=one[:], func=ACT.Sqrt)
+        make_identity(nc, ident_f[:])
+        make_identity(nc, ident_b[:])
+
+        wtmp = stage.tile([P, 8192], BF16, tag="stage", name="wtmp", align_bytes=64)
+        itmp = stage.tile([P, 8192], BF16, tag="stage", name="itmp", align_bytes=64)
+        nc.vector.memset(itmp[:, 4096:8192].bitcast(I32), 0)
+        nc.vector.tensor_scalar(out=negr[:], in0=rad_b[:], scalar1=-1.0, scalar2=None, op0=ALU.mult)
+
+        w_codes = keep.tile([P, D], U32, name="w_codes", align_bytes=64)
+        w_scales = keep.tile([P, D], U8, name="w_scales", align_bytes=64)
+        in_codes = keep.tile([P, 1024], U32, name="in_codes", align_bytes=64)
+        in_scales = keep.tile([P, 1024], U8, name="in_scales", align_bytes=64)
+
+        dist = [dpool.tile([P, COLS], F32, name="dist%d" % i) for i in range(NCH)]
+        mraw = {}
+
+        def load_mask(h):
+            t = mraw_pool.tile([P, 4, A], BF16, tag="mraw", name="mraw%d" % h)
+            nc.sync.dma_start(
+                out=t[:],
+                in_=mask[h // 2, (h % 2) * 512 : (h % 2 + 1) * 512, :].rearrange("(j p) a -> p j a", p=P),
+            )
+            mraw[h] = t
+
+        with tc.tile_pool(name="dm", bufs=6) as dmp, tc.tile_pool(name="sq", bufs=4) as sqp, tc.psum_pool(
+            name="pps", bufs=4
+        ) as pps:
+            dm = {}
+            sq = {}
+            st = {}
+
+            def load_dm(i):
+                t = dmp.tile([P, A * XD], BF16, tag="dm", name="dm%d" % i)
+                nc.sync.dma_start(
+                    out=t[:], in_=diff[i // CPN, (i % CPN) * CH : (i % CPN + 1) * CH].rearrange("b a x -> b (a x)")
+                )
+                dm[i] = t
+
+            def squares(i):
+                v = dm[i][:].rearrange("p (a x) -> p x a", x=XD)
+                s = sqp.tile([P, XD, A], F32, tag="sq", name="sq%d" % i)
+                nc.vector.tensor_tensor(out=s[:, 0, :], in0=v[:, 0, :], in1=v[:, 0, :], op=ALU.mult)
+                nc.vector.tensor_tensor(out=s[:, 1, 0:256], in0=v[:, 1, 0:256], in1=v[:, 1, 0:256], op=ALU.mult)
+                nc.scalar.activation(out=s[:, 1, 256:512], in_=v[:, 1, 256:512], func=ACT.Square)
+                nc.scalar.activation(out=s[:, 2, 0:128], in_=v[:, 2, 0:128], func=ACT.Square)
+                nc.gpsimd.tensor_tensor(out=s[:, 2, 128:512], in0=v[:, 2, 128:512], in1=v[:, 2, 128:512], op=ALU.mult)
+                sq[i] = s
+
+            def sum_transpose(i):
+                t_ps = pps.tile([P, NT, CH], F32, tag="st", name="st%d" % i)
+                for t in range(NT):
+                    for x in range(XD):
+                        nc.tensor.matmul(
+                            out=t_ps[:, t, :],
+                            lhsT=sq[i][:, x, t * P : (t + 1) * P],
+                            rhs=ident_f[:],
+                            is_transpose=True,
+                            start=(x == 0),
+                            stop=(x == XD - 1),
+                        )
+                st[i] = t_ps
+
+            def root(i):
+                nc.scalar.activation(
+                    out=dist[i][:].rearrange("p (b t) -> p b t", t=NT),
+                    in_=st[i][:].rearrange("p t b -> p b t"),
+                    func=ACT.Sqrt,
+                )
+
+            for i in range(5):
+                load_dm(i)
+            for i in range(NCH + 2):
+                if i + 5 < NCH:
+                    load_dm(i + 5)
+                if i < NCH:
+                    squares(i)
+                if 1 <= i <= NCH:
+                    sum_transpose(i - 1)
+                if i >= 2:
+                    root(i - 2)
+
+            nc.sync.dma_start(
+                out=itmp[:, 0:1024].rearrange("p (j a) -> p j a", j=2),
+                in_=feat.rearrange("n c a -> (n c) a").rearrange("(j p) a -> p j a", p=P),
+            )
+            nc.sync.dma_start(
+                out=wtmp[:, 0:4096].rearrange("p (e k) -> p e k", e=8),
+                in_=w.rearrange("(e p) c r -> p e (c r)", p=P),
+            )
+            for h in range(3):
+                load_mask(h)
+
+            inq = itmp[:, 4096:8192].rearrange("p (n h c two t) -> p n h c two t", n=NCLOUD, h=2, c=C, two=2)
+            for j in range(2):
+                ips = pps.tile([P, NT, P], BF16, tag="prep", name="ips%d" % j, bufs=3)
+                for t in range(NT):
+                    nc.tensor.transpose(
+                        out=ips[:, t, :], in_=itmp[:, j * 512 + t * P : j * 512 + (t + 1) * P], identity=ident_b[:]
+                    )
+                for n2 in range(2):
+                    for h in range(2):
+                        nc.vector.tensor_copy(
+                            out=inq[:, 2 * j + n2, h, :, h, :],
+                            in_=ips[:, :, n2 * C : (n2 + 1) * C].rearrange("p t c -> p c t"),
+                        )
+            w_words = wtmp[:, 0:4096].bitcast(F32).rearrange("p (e q u) -> p e u q", e=8, u=2)
+            w_grouped = wtmp[:, 4096:8192].bitcast(F32).rearrange("p (e d u) -> p e d u", e=8, u=2)
+            for k in range(4):
+                wps = pps.tile([P, 2, 2, P], F32, tag="prep", name="wps%d" % k, bufs=3)
+                for e in range(2):
+                    for u in range(2):
+                        nc.tensor.transpose(out=wps[:, e, u, :], in_=w_words[:, 2 * k + e, u, :], identity=ident_f[:])
+                nc.vector.tensor_copy(
+                    out=w_grouped[:, 2 * k : 2 * k + 2, :, :], in_=wps[:].rearrange("p e u d -> p e d u")
+                )
+                if k == 0:
+                    nc.vector.quantize_mx(
+                        out=in_codes[:].bitcast(FP8X4), scales=in_scales[:], in_=itmp[:, 4096:8192]
+                    )
+            nc.vector.quantize_mx(out=w_codes[:].bitcast(FP8X4), scales=w_scales[:], in_=wtmp[:, 4096:8192])
+
+        zp = ctx.enter_context(tc.tile_pool(name="z", bufs=3))
+        yp = ctx.enter_context(tc.tile_pool(name="y", bufs=2))
+        rp = ctx.enter_context(tc.tile_pool(name="r", bufs=2))
+        tp = ctx.enter_context(tc.tile_pool(name="t", bufs=2))
+        ps_m = ctx.enter_context(tc.psum_pool(name="ps_m", bufs=3))
+        ps_t = ctx.enter_context(tc.psum_pool(name="ps_t", bufs=2))
+        ps_o = ctx.enter_context(tc.psum_pool(name="ps_o", bufs=1))
+
+        z = {}
+        mt = {}
+        rb = {}
+        rc = {}
+        tps = {}
+        tb = {}
+        tcd = {}
+        ops = {}
+        sto = {}
+        G_RADII = NR - S_RADII
+
+        def pool_squares(i):
+            zt = zp.tile([P, NR, COLS], F32, tag="z", name="z%d" % i)
+            y = yp.tile([P, G_RADII, COLS], F32, tag="y", name="y%d" % i)
+            for g in range(G_RADII):
+                r = S_RADII + g
+                nc.gpsimd.tensor_scalar(
+                    out=y[:, g, :], in0=dist[i][:], scalar1=negr[:, r : r + 1], scalar2=1.0, op0=ALU.add, op1=ALU.mult
+                )
+            nc.gpsimd.tensor_tensor(out=zt[:, S_RADII:NR, :], in0=y[:], in1=y[:], op=ALU.mult)
+            z[i] = zt
+
+        def act_squares(i):
+            for r in range(S_RADII):
+                nc.scalar.activation(
+                    out=z[i][:, r, :], in_=dist[i][:], func=ACT.Square, bias=negr[:, r : r + 1], scale=1.0
+                )
+
+        def act_exp(i, h):
+            nc.scalar.activation(
+                out=z[i][:, 4 * h : 4 * h + 4, :], in_=z[i][:, 4 * h : 4 * h + 4, :], func=ACT.Exp, scale=-GAMMA
+            )
+
+        def mask_transpose(i):
+            m = ps_m.tile([P, NT, CH], BF16, tag="mt", name="mt%d" % i)
+            for t in range(NT):
+                nc.tensor.transpose(
+                    out=m[:, t, :], in_=mraw[i // 4][:, i % 4, t * P : (t + 1) * P], identity=ident_b[:]
+                )
+            mt[i] = m
+
+        def weigh(i, h):
+            if h == 0:
+                rb[i] = rp.tile([P, NR * COLS], BF16, tag="rb", name="rb%d" % i, align_bytes=64)
+            nc.vector.tensor_tensor(
+                out=rb[i][:, h * 2048 : (h + 1) * 2048].rearrange("p (b r t) -> p b r t", r=4, t=NT),
+                in0=z[i][:, 4 * h : 4 * h + 4, :].rearrange("p r (b t) -> p b r t", t=NT),
+                in1=mt[i][:].rearrange("p t b -> p b t").unsqueeze(2).to_broadcast([P, CH, 4, NT]),
+                op=ALU.mult,
+            )
+
+        def quant_r(i):
+            codes = rp.tile([P, 1024], U32, tag="rc", name="rc%d" % i, align_bytes=64)
+            scales = rp.tile([P, 1024], U8, tag="rs", name="rs%d" % i, align_bytes=64)
+            nc.vector.quantize_mx(out=codes[:].bitcast(FP8X4), scales=scales[:], in_=rb[i][:])
+            rc[i] = (codes, scales)
+
+        def matmul_one(i):
+            n = i // CPN
+            acc = ps_t.tile([P, 512], F32, tag="tps", name="tps%d" % i)
+            codes, scales = rc[i]
+            for h in range(2):
+                lo = (2 * n + h) * P
+                nc.tensor.matmul_mx(
+                    out=acc[:],
+                    lhsT=in_codes[:, lo : lo + P].bitcast(FP8X4),
+                    lhsT_scale=in_scales[:, lo : lo + P],
+                    rhs=codes[:, h * 512 : (h + 1) * 512].bitcast(FP8X4),
+                    rhs_scale=scales[:, h * 512 : (h + 1) * 512],
+                    start=(h == 0),
+                    stop=(h == 1),
+                )
+            tps[i] = acc
+
+        def t_out(i):
+            t = tp.tile([P, 512], BF16, tag="tb", name="tb%d" % i, align_bytes=64)
+            nc.vector.tensor_copy(out=t[:], in_=tps[i][:])
+            tb[i] = t
+
+        def quant_t(i):
+            codes = tp.tile([P, CH], U32, tag="tc", name="tc%d" % i, align_bytes=64)
+            scales = tp.tile([P, CH], U8, tag="ts", name="ts%d" % i, align_bytes=64)
+            nc.vector.quantize_mx(out=codes[:].bitcast(FP8X4), scales=scales[:], in_=tb[i][:])
+            tcd[i] = (codes, scales)
+
+        def matmul_two(i):
+            codes, scales = tcd[i]
+            banks = []
+            for k in range(2):
+                o = ps_o.tile([P, 4, CH], F32, tag="o%d" % k, name="o%d_%d" % (k, i))
+                for e in range(4):
+                    lo = (4 * k + e) * P
+                    nc.tensor.matmul_mx(
+                        out=o[:, e, :],
+                        lhsT=w_codes[:, lo : lo + P].bitcast(FP8X4),
+                        lhsT_scale=w_scales[:, lo : lo + P],
+                        rhs=codes[:].bitcast(FP8X4),
+                        rhs_scale=scales[:],
+                        start=True,
+                        stop=True,
+                    )
+                banks.append(o)
+            ops[i] = banks
+
+        def o_out(i):
+            hf = i // 4
+            if i % 4 == 0:
+                sto[hf] = stage.tile([P, 8, 512], F32, tag="stage", name="sto%d" % hf, align_bytes=64)
+            for k in range(2):
+                nc.vector.tensor_copy(
+                    out=sto[hf][:, 4 * k : 4 * k + 4, (i % 4) * CH : (i % 4 + 1) * CH], in_=ops[i][k][:]
+                )
+            if i % 4 == 3:
+                nc.sync.dma_start(
+                    out=out[hf // 2].rearrange("(e p) b -> p e b", p=P)[:, :, (hf % 2) * 512 : (hf % 2 + 1) * 512],
+                    in_=sto[hf][:],
+                )
+
+        pool_squares(0)
+        mask_transpose(0)
+        for i in range(NCH + 1):
+            if i + 1 < NCH:
+                pool_squares(i + 1)
+            if i < NCH:
+                act_squares(i)
+                act_exp(i, 0)
+                act_exp(i, 1)
+            if i >= 1:
+                matmul_one(i - 1)
+            if i + 1 < NCH:
+                mask_transpose(i + 1)
+            if i % 4 == 3 and i // 4 + 3 < 8:
+                load_mask(i // 4 + 3)
+            if i < NCH:
+                weigh(i, 0)
+            if i >= 1:
+                t_out(i - 1)
+            if i < NCH:
+                weigh(i, 1)
+            if i >= 1:
+                quant_t(i - 1)
+                matmul_two(i - 1)
+            if i < NCH:
+                quant_r(i)
+            if i >= 1:
+                o_out(i - 1)

@@ -89,21 +89,23 @@ def tile_se3pointconvolution_t_kernel(tc, feat, diff, mask, w, radii, out):
                 nc.vector.tensor_tensor(out=s[:, 0, :], in0=v[:, 0, :], in1=v[:, 0, :], op=ALU.mult)
                 nc.vector.tensor_tensor(out=s[:, 1, 0:256], in0=v[:, 1, 0:256], in1=v[:, 1, 0:256], op=ALU.mult)
                 nc.scalar.activation(out=s[:, 1, 256:512], in_=v[:, 1, 256:512], func=ACT.Square)
-                nc.scalar.activation(out=s[:, 2, 0:128], in_=v[:, 2, 0:128], func=ACT.Square)
-                nc.gpsimd.tensor_tensor(out=s[:, 2, 128:512], in0=v[:, 2, 128:512], in1=v[:, 2, 128:512], op=ALU.mult)
+                nc.scalar.activation(out=s[:, 2, :], in_=v[:, 2, :], func=ACT.Square)
                 sq[i] = s
+
+            def add_planes(i):
+                nc.vector.tensor_tensor(out=sq[i][:, 0, :], in0=sq[i][:, 0, :], in1=sq[i][:, 1, :], op=ALU.add)
 
             def sum_transpose(i):
                 t_ps = pps.tile([P, NT, CH], F32, tag="st", name="st%d" % i)
                 for t in range(NT):
-                    for x in range(XD):
+                    for x in (0, 2):
                         nc.tensor.matmul(
                             out=t_ps[:, t, :],
                             lhsT=sq[i][:, x, t * P : (t + 1) * P],
                             rhs=ident_f[:],
                             is_transpose=True,
                             start=(x == 0),
-                            stop=(x == XD - 1),
+                            stop=(x == 2),
                         )
                 st[i] = t_ps
 
@@ -122,6 +124,7 @@ def tile_se3pointconvolution_t_kernel(tc, feat, diff, mask, w, radii, out):
                 if i < NCH:
                     squares(i)
                 if 1 <= i <= NCH:
+                    add_planes(i - 1)
                     sum_transpose(i - 1)
                 if i >= 2:
                     root(i - 2)
@@ -170,9 +173,9 @@ def tile_se3pointconvolution_t_kernel(tc, feat, diff, mask, w, radii, out):
         yp = ctx.enter_context(tc.tile_pool(name="y", bufs=2))
         rp = ctx.enter_context(tc.tile_pool(name="r", bufs=2))
         tp = ctx.enter_context(tc.tile_pool(name="t", bufs=2))
-        ps_m = ctx.enter_context(tc.psum_pool(name="ps_m", bufs=3))
+        ps_m = ctx.enter_context(tc.psum_pool(name="ps_m", bufs=2))
         ps_t = ctx.enter_context(tc.psum_pool(name="ps_t", bufs=2))
-        ps_o = ctx.enter_context(tc.psum_pool(name="ps_o", bufs=1))
+        ps_o = ctx.enter_context(tc.psum_pool(name="ps_o", bufs=2))
 
         z = {}
         mt = {}
@@ -278,30 +281,33 @@ def tile_se3pointconvolution_t_kernel(tc, feat, diff, mask, w, radii, out):
                 banks.append(o)
             ops[i] = banks
 
-        def o_out(i):
+        def o_out(i, engines):
             hf = i // 4
             if i % 4 == 0:
                 sto[hf] = stage.tile([P, 8, 512], F32, tag="stage", name="sto%d" % hf, align_bytes=64)
+            cols = slice((i % 4) * CH, (i % 4 + 1) * CH)
             for k in range(2):
-                nc.vector.tensor_copy(
-                    out=sto[hf][:, 4 * k : 4 * k + 4, (i % 4) * CH : (i % 4 + 1) * CH], in_=ops[i][k][:]
-                )
-            if i % 4 == 3:
-                nc.sync.dma_start(
-                    out=out[hf // 2].rearrange("(e p) b -> p e b", p=P)[:, :, (hf % 2) * 512 : (hf % 2 + 1) * 512],
-                    in_=sto[hf][:],
-                )
+                if engines[k] == "v":
+                    nc.vector.tensor_copy(out=sto[hf][:, 4 * k : 4 * k + 4, cols], in_=ops[i][k][:])
+                else:
+                    nc.scalar.copy(out=sto[hf][:, 4 * k : 4 * k + 4, cols], in_=ops[i][k][:])
+            dst = out[hf // 2].rearrange("(e p) b -> p e b", p=P)
+            base = (hf % 2) * 512
+            if hf == 7:
+                nc.sync.dma_start(out=dst[:, :, base + (i % 4) * CH : base + (i % 4 + 1) * CH], in_=sto[hf][:, :, cols])
+            elif i % 4 == 3:
+                nc.sync.dma_start(out=dst[:, :, base : base + 512], in_=sto[hf][:])
 
         pool_squares(0)
         mask_transpose(0)
-        for i in range(NCH + 1):
+        for i in range(NCH + 2):
             if i + 1 < NCH:
                 pool_squares(i + 1)
             if i < NCH:
                 act_squares(i)
                 act_exp(i, 0)
                 act_exp(i, 1)
-            if i >= 1:
+            if 1 <= i <= NCH:
                 matmul_one(i - 1)
             if i + 1 < NCH:
                 mask_transpose(i + 1)
@@ -309,14 +315,14 @@ def tile_se3pointconvolution_t_kernel(tc, feat, diff, mask, w, radii, out):
                 load_mask(i // 4 + 3)
             if i < NCH:
                 weigh(i, 0)
-            if i >= 1:
+            if 1 <= i <= NCH:
                 t_out(i - 1)
             if i < NCH:
                 weigh(i, 1)
-            if i >= 1:
+            if 1 <= i <= NCH:
                 quant_t(i - 1)
                 matmul_two(i - 1)
             if i < NCH:
                 quant_r(i)
-            if i >= 1:
-                o_out(i - 1)
+            if i >= 2:
+                o_out(i - 2, "vv" if i < NCH - 1 else ("ss" if i <= NCH else "vs"))

@@ -22,7 +22,12 @@ CH = 128
 CPN = B // CH
 NCH = NCLOUD * CPN
 COLS = CH * NT
-S_RADII = 5
+
+
+def scalar_radii(i):
+    return 6 if i % 4 == 3 else 5
+
+
 FLOPS = 2 * NCLOUD * C * A * B * NR + 2 * NCLOUD * D * C * NR * B
 
 
@@ -169,7 +174,7 @@ def tile_se3pointconvolution_t_kernel(tc, feat, diff, mask, w, radii, out):
                     )
             nc.vector.quantize_mx(out=w_codes[:].bitcast(FP8X4), scales=w_scales[:], in_=wtmp[:, 4096:8192])
 
-        zp = ctx.enter_context(tc.tile_pool(name="z", bufs=3))
+        zp = ctx.enter_context(tc.tile_pool(name="z", bufs=4))
         yp = ctx.enter_context(tc.tile_pool(name="y", bufs=2))
         rp = ctx.enter_context(tc.tile_pool(name="r", bufs=2))
         tp = ctx.enter_context(tc.tile_pool(name="t", bufs=2))
@@ -186,21 +191,27 @@ def tile_se3pointconvolution_t_kernel(tc, feat, diff, mask, w, radii, out):
         tcd = {}
         ops = {}
         sto = {}
-        G_RADII = NR - S_RADII
 
         def pool_squares(i):
+            first = scalar_radii(i)
             zt = zp.tile([P, NR, COLS], F32, tag="z", name="z%d" % i)
-            y = yp.tile([P, G_RADII, COLS], F32, tag="y", name="y%d" % i)
-            for g in range(G_RADII):
-                r = S_RADII + g
+            y = yp.tile([P, 3, COLS], F32, tag="y", name="y%d" % i)
+            for r in range(first, NR):
                 nc.gpsimd.tensor_scalar(
-                    out=y[:, g, :], in0=dist[i][:], scalar1=negr[:, r : r + 1], scalar2=1.0, op0=ALU.add, op1=ALU.mult
+                    out=y[:, r - first, :],
+                    in0=dist[i][:],
+                    scalar1=negr[:, r : r + 1],
+                    scalar2=1.0,
+                    op0=ALU.add,
+                    op1=ALU.mult,
                 )
-            nc.gpsimd.tensor_tensor(out=zt[:, S_RADII:NR, :], in0=y[:], in1=y[:], op=ALU.mult)
+            nc.gpsimd.tensor_tensor(
+                out=zt[:, first:NR, :], in0=y[:, 0 : NR - first, :], in1=y[:, 0 : NR - first, :], op=ALU.mult
+            )
             z[i] = zt
 
         def act_squares(i):
-            for r in range(S_RADII):
+            for r in range(scalar_radii(i)):
                 nc.scalar.activation(
                     out=z[i][:, r, :], in_=dist[i][:], func=ACT.Square, bias=negr[:, r : r + 1], scale=1.0
                 )

@@ -25,7 +25,7 @@ COLS = CH * NT
 
 
 def scalar_radii(i):
-    return 6 if i % 4 == 3 else 5
+    return 5
 
 
 FLOPS = 2 * NCLOUD * C * A * B * NR + 2 * NCLOUD * D * C * NR * B
@@ -292,28 +292,51 @@ def tile_se3pointconvolution_t_kernel(tc, feat, diff, mask, w, radii, out):
                 banks.append(o)
             ops[i] = banks
 
-        def o_out(i, engines):
+        def o_plan(i):
+            if i == NCH - 1:
+                return (("v", 2), ("s", 2))
+            if i >= NCH - 3:
+                return (("s", 2), ("s", 2))
+            if i % 2 == 1:
+                return (("v", 2), ("s", 4))
+            return (("v", 2), ("v", 2))
+
+        def o_bank(i, k, engine):
             hf = i // 4
-            if i % 4 == 0:
+            if i % 4 == 0 and k == 0:
                 sto[hf] = stage.tile([P, 8, 512], F32, tag="stage", name="sto%d" % hf, align_bytes=64)
             cols = slice((i % 4) * CH, (i % 4 + 1) * CH)
-            for k in range(2):
-                if engines[k] == "v":
-                    nc.vector.tensor_copy(out=sto[hf][:, 4 * k : 4 * k + 4, cols], in_=ops[i][k][:])
-                else:
-                    nc.scalar.copy(out=sto[hf][:, 4 * k : 4 * k + 4, cols], in_=ops[i][k][:])
+            if engine == "v":
+                nc.vector.tensor_copy(out=sto[hf][:, 4 * k : 4 * k + 4, cols], in_=ops[i][k][:])
+            else:
+                nc.scalar.copy(out=sto[hf][:, 4 * k : 4 * k + 4, cols], in_=ops[i][k][:])
+
+        def store(i):
+            hf = i // 4
             dst = out[hf // 2].rearrange("(e p) b -> p e b", p=P)
             base = (hf % 2) * 512
+            lo = (i % 4) * CH
             if hf == 7:
-                nc.sync.dma_start(out=dst[:, :, base + (i % 4) * CH : base + (i % 4 + 1) * CH], in_=sto[hf][:, :, cols])
+                nc.sync.dma_start(out=dst[:, :, base + lo : base + lo + CH], in_=sto[hf][:, :, lo : lo + CH])
             elif i % 4 == 3:
                 nc.sync.dma_start(out=dst[:, :, base : base + 512], in_=sto[hf][:])
+
+        def o_step(i, lag):
+            j = i - lag
+            if 0 <= j < NCH:
+                plan = o_plan(j)
+                for k in range(2):
+                    if plan[k][1] == lag:
+                        o_bank(j, k, plan[k][0])
+                if max(plan[0][1], plan[1][1]) == lag:
+                    store(j)
 
         pool_squares(0)
         mask_transpose(0)
         for i in range(NCH + 2):
             if i + 1 < NCH:
                 pool_squares(i + 1)
+            o_step(i, 4)
             if i < NCH:
                 act_squares(i)
                 act_exp(i, 0)
@@ -335,5 +358,4 @@ def tile_se3pointconvolution_t_kernel(tc, feat, diff, mask, w, radii, out):
                 matmul_two(i - 1)
             if i < NCH:
                 quant_r(i)
-            if i >= 2:
-                o_out(i - 2, "vv" if i < NCH - 1 else ("ss" if i <= NCH else "vs"))
+            o_step(i, 2)

@@ -22,12 +22,7 @@ CH = 128
 CPN = B // CH
 NCH = NCLOUD * CPN
 COLS = CH * NT
-
-
-def scalar_radii(i):
-    return 5
-
-
+S_RADII = 5
 FLOPS = 2 * NCLOUD * C * A * B * NR + 2 * NCLOUD * D * C * NR * B
 
 
@@ -48,7 +43,9 @@ def tile_se3pointconvolution_t_kernel(tc, feat, diff, mask, w, radii, out):
         ident_f = const.tile([P, P], F32, name="ident_f")
         ident_b = const.tile([P, P], BF16, name="ident_b")
         nc.scalar.dma_start(out=rad_b[:], in_=radii.partition_broadcast(P))
+        zeros = const.tile([P, 512], BF16, name="zeros")
         nc.vector.memset(one[:], 1.0)
+        nc.vector.memset(zeros[:], 0.0)
         nc.scalar.activation(out=junk[:], in_=one[:], func=ACT.Sqrt)
         make_identity(nc, ident_f[:])
         make_identity(nc, ident_b[:])
@@ -91,27 +88,26 @@ def tile_se3pointconvolution_t_kernel(tc, feat, diff, mask, w, radii, out):
             def squares(i):
                 v = dm[i][:].rearrange("p (a x) -> p x a", x=XD)
                 s = sqp.tile([P, XD, A], F32, tag="sq", name="sq%d" % i)
-                nc.vector.tensor_tensor(out=s[:, 0, :], in0=v[:, 0, :], in1=v[:, 0, :], op=ALU.mult)
-                nc.vector.tensor_tensor(out=s[:, 1, 0:256], in0=v[:, 1, 0:256], in1=v[:, 1, 0:256], op=ALU.mult)
-                nc.scalar.activation(out=s[:, 1, 256:512], in_=v[:, 1, 256:512], func=ACT.Square)
+                nc.vector.tensor_tensor(out=s[:, 0:2, :], in0=v[:, 0:2, :], in1=v[:, 0:2, :], op=ALU.mult)
                 nc.scalar.activation(out=s[:, 2, :], in_=v[:, 2, :], func=ACT.Square)
                 sq[i] = s
 
-            def add_planes(i):
-                nc.vector.tensor_tensor(out=sq[i][:, 0, :], in0=sq[i][:, 0, :], in1=sq[i][:, 1, :], op=ALU.add)
+            def keep_clock(n):
+                nc.tensor.matmul(out=warm[:, 0:n], lhsT=ident_b[:], rhs=zeros[:, 0:n], start=True, stop=True)
 
             def sum_transpose(i):
                 t_ps = pps.tile([P, NT, CH], F32, tag="st", name="st%d" % i)
                 for t in range(NT):
-                    for x in (0, 2):
+                    for x in range(XD):
                         nc.tensor.matmul(
                             out=t_ps[:, t, :],
                             lhsT=sq[i][:, x, t * P : (t + 1) * P],
                             rhs=ident_f[:],
                             is_transpose=True,
                             start=(x == 0),
-                            stop=(x == 2),
+                            stop=(x == XD - 1),
                         )
+                keep_clock(256)
                 st[i] = t_ps
 
             def root(i):
@@ -121,15 +117,17 @@ def tile_se3pointconvolution_t_kernel(tc, feat, diff, mask, w, radii, out):
                     func=ACT.Sqrt,
                 )
 
+            warm = pps.tile([P, 512], F32, tag="warm", name="warm", bufs=1)
             for i in range(5):
                 load_dm(i)
+            for i in range(8):
+                keep_clock(512)
             for i in range(NCH + 2):
                 if i + 5 < NCH:
                     load_dm(i + 5)
                 if i < NCH:
                     squares(i)
                 if 1 <= i <= NCH:
-                    add_planes(i - 1)
                     sum_transpose(i - 1)
                 if i >= 2:
                     root(i - 2)
@@ -191,27 +189,21 @@ def tile_se3pointconvolution_t_kernel(tc, feat, diff, mask, w, radii, out):
         tcd = {}
         ops = {}
         sto = {}
+        G_RADII = NR - S_RADII
 
         def pool_squares(i):
-            first = scalar_radii(i)
             zt = zp.tile([P, NR, COLS], F32, tag="z", name="z%d" % i)
-            y = yp.tile([P, 3, COLS], F32, tag="y", name="y%d" % i)
-            for r in range(first, NR):
+            y = yp.tile([P, G_RADII, COLS], F32, tag="y", name="y%d" % i)
+            for g in range(G_RADII):
+                r = S_RADII + g
                 nc.gpsimd.tensor_scalar(
-                    out=y[:, r - first, :],
-                    in0=dist[i][:],
-                    scalar1=negr[:, r : r + 1],
-                    scalar2=1.0,
-                    op0=ALU.add,
-                    op1=ALU.mult,
+                    out=y[:, g, :], in0=dist[i][:], scalar1=negr[:, r : r + 1], scalar2=1.0, op0=ALU.add, op1=ALU.mult
                 )
-            nc.gpsimd.tensor_tensor(
-                out=zt[:, first:NR, :], in0=y[:, 0 : NR - first, :], in1=y[:, 0 : NR - first, :], op=ALU.mult
-            )
+            nc.gpsimd.tensor_tensor(out=zt[:, S_RADII:NR, :], in0=y[:], in1=y[:], op=ALU.mult)
             z[i] = zt
 
         def act_squares(i):
-            for r in range(scalar_radii(i)):
+            for r in range(S_RADII):
                 nc.scalar.activation(
                     out=z[i][:, r, :], in_=dist[i][:], func=ACT.Square, bias=negr[:, r : r + 1], scale=1.0
                 )
@@ -292,51 +284,28 @@ def tile_se3pointconvolution_t_kernel(tc, feat, diff, mask, w, radii, out):
                 banks.append(o)
             ops[i] = banks
 
-        def o_plan(i):
-            if i == NCH - 1:
-                return (("v", 2), ("s", 2))
-            if i >= NCH - 3:
-                return (("s", 2), ("s", 2))
-            if i % 2 == 1:
-                return (("v", 2), ("s", 4))
-            return (("v", 2), ("v", 2))
-
-        def o_bank(i, k, engine):
+        def o_out(i, engines):
             hf = i // 4
-            if i % 4 == 0 and k == 0:
+            if i % 4 == 0:
                 sto[hf] = stage.tile([P, 8, 512], F32, tag="stage", name="sto%d" % hf, align_bytes=64)
             cols = slice((i % 4) * CH, (i % 4 + 1) * CH)
-            if engine == "v":
-                nc.vector.tensor_copy(out=sto[hf][:, 4 * k : 4 * k + 4, cols], in_=ops[i][k][:])
-            else:
-                nc.scalar.copy(out=sto[hf][:, 4 * k : 4 * k + 4, cols], in_=ops[i][k][:])
-
-        def store(i):
-            hf = i // 4
+            for k in range(2):
+                if engines[k] == "v":
+                    nc.vector.tensor_copy(out=sto[hf][:, 4 * k : 4 * k + 4, cols], in_=ops[i][k][:])
+                else:
+                    nc.scalar.copy(out=sto[hf][:, 4 * k : 4 * k + 4, cols], in_=ops[i][k][:])
             dst = out[hf // 2].rearrange("(e p) b -> p e b", p=P)
             base = (hf % 2) * 512
-            lo = (i % 4) * CH
             if hf == 7:
-                nc.sync.dma_start(out=dst[:, :, base + lo : base + lo + CH], in_=sto[hf][:, :, lo : lo + CH])
+                nc.sync.dma_start(out=dst[:, :, base + (i % 4) * CH : base + (i % 4 + 1) * CH], in_=sto[hf][:, :, cols])
             elif i % 4 == 3:
                 nc.sync.dma_start(out=dst[:, :, base : base + 512], in_=sto[hf][:])
-
-        def o_step(i, lag):
-            j = i - lag
-            if 0 <= j < NCH:
-                plan = o_plan(j)
-                for k in range(2):
-                    if plan[k][1] == lag:
-                        o_bank(j, k, plan[k][0])
-                if max(plan[0][1], plan[1][1]) == lag:
-                    store(j)
 
         pool_squares(0)
         mask_transpose(0)
         for i in range(NCH + 2):
             if i + 1 < NCH:
                 pool_squares(i + 1)
-            o_step(i, 4)
             if i < NCH:
                 act_squares(i)
                 act_exp(i, 0)
@@ -358,4 +327,5 @@ def tile_se3pointconvolution_t_kernel(tc, feat, diff, mask, w, radii, out):
                 matmul_two(i - 1)
             if i < NCH:
                 quant_r(i)
-            o_step(i, 2)
+            if i >= 2:
+                o_out(i - 2, "vv" if i < NCH - 1 else ("ss" if i <= NCH else "vs"))

from contextlib import ExitStack

import concourse.bass as bass
import concourse.mybir as mybir
import concourse.tile as tile
from concourse.masks import make_identity

F32 = mybir.dt.float32
BF16 = mybir.dt.bfloat16
U32 = mybir.dt.uint32
U8 = mybir.dt.uint8
I32 = mybir.dt.int32
FP8X4 = mybir.dt.float8_e4m3fn_x4
ACT = mybir.ActivationFunctionType
ALU = mybir.AluOpType

NCLOUD, B, A, C, D, NR, XD = 4, 1024, 512, 64, 1024, 8, 3
GAMMA = 6.125
P = 128
NT = A // P
CH = 128
CPN = B // CH
NCH = NCLOUD * CPN
COLS = CH * NT
S_RADII = 5
FLOPS = 2 * NCLOUD * C * A * B * NR + 2 * NCLOUD * D * C * NR * B


def tile_se3pointconvolution_t_kernel(tc, feat, diff, mask, w, radii, out):
    nc = tc.nc
    with ExitStack() as ctx:
        ctx.enter_context(tc.manual_schedule())
        const = ctx.enter_context(tc.tile_pool(name="const", bufs=1))
        dpool = ctx.enter_context(tc.tile_pool(name="dist", bufs=1))
        keep = ctx.enter_context(tc.tile_pool(name="keep", bufs=1))
        stage = ctx.enter_context(tc.tile_pool(name="stage", bufs=2))
        mraw_pool = ctx.enter_context(tc.tile_pool(name="mraw", bufs=3))

        one = const.tile([P, 1], F32, name="one")
        junk = const.tile([P, 1], F32, name="junk")
        rad_b = const.tile([P, NR], BF16, name="rad_b")
        negr = const.tile([P, NR], F32, name="negr")
        ident_f = const.tile([P, P], F32, name="ident_f")
        ident_b = const.tile([P, P], BF16, name="ident_b")
        nc.scalar.dma_start(out=rad_b[:], in_=radii.partition_broadcast(P))
        zeros = const.tile([P, 512], BF16, name="zeros")
        nc.vector.memset(one[:], 1.0)
        nc.vector.memset(zeros[:], 0.0)
        nc.scalar.activation(out=junk[:], in_=one[:], func=ACT.Sqrt)
        make_identity(nc, ident_f[:])
        make_identity(nc, ident_b[:])

        wtmp = stage.tile([P, 8192], BF16, tag="stage", name="wtmp", align_bytes=64)
        itmp = stage.tile([P, 8192], BF16, tag="stage", name="itmp", align_bytes=64)
        nc.vector.memset(itmp[:, 4096:8192].bitcast(I32), 0)
        nc.vector.tensor_scalar(out=negr[:], in0=rad_b[:], scalar1=-1.0, scalar2=None, op0=ALU.mult)

        w_codes = keep.tile([P, D], U32, name="w_codes", align_bytes=64)
        w_scales = keep.tile([P, D], U8, name="w_scales", align_bytes=64)
        in_codes = keep.tile([P, 1024], U32, name="in_codes", align_bytes=64)
        in_scales = keep.tile([P, 1024], U8, name="in_scales", align_bytes=64)

        dist = [dpool.tile([P, COLS], F32, name="dist%d" % i) for i in range(NCH)]
        mraw = {}

        def load_mask(h):
            t = mraw_pool.tile([P, 4, A], BF16, tag="mraw", name="mraw%d" % h)
            nc.sync.dma_start(
                out=t[:],
                in_=mask[h // 2, (h % 2) * 512 : (h % 2 + 1) * 512, :].rearrange("(j p) a -> p j a", p=P),
            )
            mraw[h] = t

        with tc.tile_pool(name="dm", bufs=6) as dmp, tc.tile_pool(name="sq", bufs=4) as sqp, tc.psum_pool(
            name="pps", bufs=4
        ) as pps:
            dm = {}
            sq = {}
            st = {}

            def load_dm(i):
                t = dmp.tile([P, A * XD], BF16, tag="dm", name="dm%d" % i)
                nc.sync.dma_start(
                    out=t[:], in_=diff[i // CPN, (i % CPN) * CH : (i % CPN + 1) * CH].rearrange("b a x -> b (a x)")
                )
                dm[i] = t

            def squares(i):
                v = dm[i][:].rearrange("p (a x) -> p x a", x=XD)
                s = sqp.tile([P, XD, A], F32, tag="sq", name="sq%d" % i)
                nc.vector.tensor_tensor(out=s[:, 0:2, :], in0=v[:, 0:2, :], in1=v[:, 0:2, :], op=ALU.mult)
                nc.scalar.activation(out=s[:, 2, :], in_=v[:, 2, :], func=ACT.Square)
                sq[i] = s

            def keep_clock(n):
                nc.tensor.matmul(out=warm[:, 0:n], lhsT=ident_b[:], rhs=zeros[:, 0:n], start=True, stop=True)

            def sum_transpose(i):
                t_ps = pps.tile([P, NT, CH], F32, tag="st", name="st%d" % i)
                for t in range(NT):
                    for x in range(XD):
                        nc.tensor.matmul(
                            out=t_ps[:, t, :],
                            lhsT=sq[i][:, x, t * P : (t + 1) * P],
                            rhs=ident_f[:],
                            is_transpose=True,
                            start=(x == 0),
                            stop=(x == XD - 1),
                        )
                keep_clock(256)
                st[i] = t_ps

            def root(i):
                nc.scalar.activation(
                    out=dist[i][:].rearrange("p (b t) -> p b t", t=NT),
                    in_=st[i][:].rearrange("p t b -> p b t"),
                    func=ACT.Sqrt,
                )

            warm = pps.tile([P, 512], F32, tag="warm", name="warm", bufs=1)
            for i in range(5):
                load_dm(i)
            for i in range(8):
                keep_clock(512)
            for i in range(NCH + 2):
                if i + 5 < NCH:
                    load_dm(i + 5)
                if i < NCH:
                    squares(i)
                if 1 <= i <= NCH:
                    sum_transpose(i - 1)
                if i >= 2:
                    root(i - 2)

            nc.sync.dma_start(
                out=itmp[:, 0:1024].rearrange("p (j a) -> p j a", j=2),
                in_=feat.rearrange("n c a -> (n c) a").rearrange("(j p) a -> p j a", p=P),
            )
            nc.sync.dma_start(
                out=wtmp[:, 0:4096].rearrange("p (e k) -> p e k", e=8),
                in_=w.rearrange("(e p) c r -> p e (c r)", p=P),
            )
            for h in range(3):
                load_mask(h)

            inq = itmp[:, 4096:8192].rearrange("p (n h c two t) -> p n h c two t", n=NCLOUD, h=2, c=C, two=2)
            for j in range(2):
                ips = pps.tile([P, NT, P], BF16, tag="prep", name="ips%d" % j, bufs=3)
                for t in range(NT):
                    nc.tensor.transpose(
                        out=ips[:, t, :], in_=itmp[:, j * 512 + t * P : j * 512 + (t + 1) * P], identity=ident_b[:]
                    )
                for n2 in range(2):
                    for h in range(2):
                        nc.vector.tensor_copy(
                            out=inq[:, 2 * j + n2, h, :, h, :],
                            in_=ips[:, :, n2 * C : (n2 + 1) * C].rearrange("p t c -> p c t"),
                        )
            w_words = wtmp[:, 0:4096].bitcast(F32).rearrange("p (e q u) -> p e u q", e=8, u=2)
            w_grouped = wtmp[:, 4096:8192].bitcast(F32).rearrange("p (e d u) -> p e d u", e=8, u=2)
            for k in range(4):
                wps = pps.tile([P, 2, 2, P], F32, tag="prep", name="wps%d" % k, bufs=3)
                for e in range(2):
                    for u in range(2):
                        nc.tensor.transpose(out=wps[:, e, u, :], in_=w_words[:, 2 * k + e, u, :], identity=ident_f[:])
                nc.vector.tensor_copy(
                    out=w_grouped[:, 2 * k : 2 * k + 2, :, :], in_=wps[:].rearrange("p e u d -> p e d u")
                )
                if k == 0:
                    nc.vector.quantize_mx(
                        out=in_codes[:].bitcast(FP8X4), scales=in_scales[:], in_=itmp[:, 4096:8192]
                    )
            nc.vector.quantize_mx(out=w_codes[:].bitcast(FP8X4), scales=w_scales[:], in_=wtmp[:, 4096:8192])

        zp = ctx.enter_context(tc.tile_pool(name="z", bufs=4))
        yp = ctx.enter_context(tc.tile_pool(name="y", bufs=2))
        rp = ctx.enter_context(tc.tile_pool(name="r", bufs=2))
        tp = ctx.enter_context(tc.tile_pool(name="t", bufs=2))
        ps_m = ctx.enter_context(tc.psum_pool(name="ps_m", bufs=2))
        ps_t = ctx.enter_context(tc.psum_pool(name="ps_t", bufs=2))
        ps_o = ctx.enter_context(tc.psum_pool(name="ps_o", bufs=2))

        z = {}
        mt = {}
        rb = {}
        rc = {}
        tps = {}
        tb = {}
        tcd = {}
        ops = {}
        sto = {}
        G_RADII = NR - S_RADII

        def pool_squares(i):
            zt = zp.tile([P, NR, COLS], F32, tag="z", name="z%d" % i)
            y = yp.tile([P, G_RADII, COLS], F32, tag="y", name="y%d" % i)
            for g in range(G_RADII):
                r = S_RADII + g
                nc.gpsimd.tensor_scalar(
                    out=y[:, g, :], in0=dist[i][:], scalar1=negr[:, r : r + 1], scalar2=1.0, op0=ALU.add, op1=ALU.mult
                )
            nc.gpsimd.tensor_tensor(out=zt[:, S_RADII:NR, :], in0=y[:], in1=y[:], op=ALU.mult)
            z[i] = zt

        def act_squares(i):
            for r in range(S_RADII):
                nc.scalar.activation(
                    out=z[i][:, r, :], in_=dist[i][:], func=ACT.Square, bias=negr[:, r : r + 1], scale=1.0
                )

        def act_exp(i, h):
            nc.scalar.activation(
                out=z[i][:, 4 * h : 4 * h + 4, :], in_=z[i][:, 4 * h : 4 * h + 4, :], func=ACT.Exp, scale=-GAMMA
            )

        def mask_transpose(i):
            m = ps_m.tile([P, NT, CH], BF16, tag="mt", name="mt%d" % i)
            for t in range(NT):
                nc.tensor.transpose(
                    out=m[:, t, :], in_=mraw[i // 4][:, i % 4, t * P : (t + 1) * P], identity=ident_b[:]
                )
            mt[i] = m

        def weigh(i, h):
            if h == 0:
                rb[i] = rp.tile([P, NR * COLS], BF16, tag="rb", name="rb%d" % i, align_bytes=64)
            nc.vector.tensor_tensor(
                out=rb[i][:, h * 2048 : (h + 1) * 2048].rearrange("p (b r t) -> p b r t", r=4, t=NT),
                in0=z[i][:, 4 * h : 4 * h + 4, :].rearrange("p r (b t) -> p b r t", t=NT),
                in1=mt[i][:].rearrange("p t b -> p b t").unsqueeze(2).to_broadcast([P, CH, 4, NT]),
                op=ALU.mult,
            )

        def quant_r(i):
            codes = rp.tile([P, 1024], U32, tag="rc", name="rc%d" % i, align_bytes=64)
            scales = rp.tile([P, 1024], U8, tag="rs", name="rs%d" % i, align_bytes=64)
            nc.vector.quantize_mx(out=codes[:].bitcast(FP8X4), scales=scales[:], in_=rb[i][:])
            rc[i] = (codes, scales)

        def matmul_one(i):
            n = i // CPN
            acc = ps_t.tile([P, 512], F32, tag="tps", name="tps%d" % i)
            codes, scales = rc[i]
            for h in range(2):
                lo = (2 * n + h) * P
                nc.tensor.matmul_mx(
                    out=acc[:],
                    lhsT=in_codes[:, lo : lo + P].bitcast(FP8X4),
                    lhsT_scale=in_scales[:, lo : lo + P],
                    rhs=codes[:, h * 512 : (h + 1) * 512].bitcast(FP8X4),
                    rhs_scale=scales[:, h * 512 : (h + 1) * 512],
                    start=(h == 0),
                    stop=(h == 1),
                )
            tps[i] = acc

        def t_out(i):
            t = tp.tile([P, 512], BF16, tag="tb", name="tb%d" % i, align_bytes=64)
            nc.vector.tensor_copy(out=t[:], in_=tps[i][:])
            tb[i] = t

        def quant_t(i):
            codes = tp.tile([P, CH], U32, tag="tc", name="tc%d" % i, align_bytes=64)
            scales = tp.tile([P, CH], U8, tag="ts", name="ts%d" % i, align_bytes=64)
            nc.vector.quantize_mx(out=codes[:].bitcast(FP8X4), scales=scales[:], in_=tb[i][:])
            tcd[i] = (codes, scales)

        def matmul_two(i):
            codes, scales = tcd[i]
            banks = []
            for k in range(2):
                o = ps_o.tile([P, 4, CH], F32, tag="o%d" % k, name="o%d_%d" % (k, i))
                for e in range(4):
                    lo = (4 * k + e) * P
                    nc.tensor.matmul_mx(
                        out=o[:, e, :],
                        lhsT=w_codes[:, lo : lo + P].bitcast(FP8X4),
                        lhsT_scale=w_scales[:, lo : lo + P],
                        rhs=codes[:].bitcast(FP8X4),
                        rhs_scale=scales[:],
                        start=True,
                        stop=True,
                    )
                banks.append(o)
            ops[i] = banks

        def o_out(i, engines):
            hf = i // 4
            if i % 4 == 0:
                sto[hf] = stage.tile([P, 8, 512], F32, tag="stage", name="sto%d" % hf, align_bytes=64)
            cols = slice((i % 4) * CH, (i % 4 + 1) * CH)
            for k in range(2):
                if engines[k] == "v":
                    nc.vector.tensor_copy(out=sto[hf][:, 4 * k : 4 * k + 4, cols], in_=ops[i][k][:])
                else:
                    nc.scalar.copy(out=sto[hf][:, 4 * k : 4 * k + 4, cols], in_=ops[i][k][:])
            dst = out[hf // 2].rearrange("(e p) b -> p e b", p=P)
            base = (hf % 2) * 512
            if hf == 7:
                nc.sync.dma_start(out=dst[:, :, base + (i % 4) * CH : base + (i % 4 + 1) * CH], in_=sto[hf][:, :, cols])
            elif i % 4 == 3:
                nc.sync.dma_start(out=dst[:, :, base : base + 512], in_=sto[hf][:])

        pool_squares(0)
        mask_transpose(0)
        for i in range(NCH + 2):
            if i + 1 < NCH:
                pool_squares(i + 1)
            if i < NCH:
                act_squares(i)
                act_exp(i, 0)
                act_exp(i, 1)
            if 1 <= i <= NCH:
                matmul_one(i - 1)
            if i + 1 < NCH:
                mask_transpose(i + 1)
            if i % 4 == 3 and i // 4 + 3 < 8:
                load_mask(i // 4 + 3)
            if i < NCH:
                weigh(i, 0)
            if 1 <= i <= NCH:
                t_out(i - 1)
            if i < NCH:
                weigh(i, 1)
            if 1 <= i <= NCH:
                quant_t(i - 1)
                matmul_two(i - 1)
            if i < NCH:
                quant_r(i)
            if i >= 2:
                o_out(i - 2, "vv" if i < NCH - 1 else ("ss" if i <= NCH else "vs"))
